import numpy as np
import ml_dtypes


def mxq(x, axis, fmt="e4m3"):
    dtype, down = {"e4m3": (ml_dtypes.float8_e4m3fn, 7), "e5m2": (ml_dtypes.float8_e5m2, 14)}[fmt]
    v = np.moveaxis(np.asarray(x, np.float32).astype(ml_dtypes.bfloat16).astype(np.float64), axis, -1)
    blocks = v.reshape(v.shape[:-1] + (-1, 32))
    amax = np.abs(blocks).max(-1, keepdims=True)
    byte = np.maximum(np.where(amax > 0, np.frexp(amax)[1] - 1 + 127, 0) - down, 1)
    scale = np.exp2(byte - 127.0)
    codes = (blocks / scale).astype(np.float32).astype(dtype).astype(np.float64)
    return np.moveaxis((codes * scale).reshape(v.shape), -1, axis)


WIDE = False


def mx_kscale(k):
    if not WIDE:
        return np.ones(k)
    levels = np.array([10, -10, 5, -5, 0])
    a = np.random.permutation(np.resize(levels, k // 512 * 4)).reshape(k // 512, 4)
    idx = np.arange(k)
    return np.exp2(a[idx // 512, idx % 128 // 32])


BF16 = ml_dtypes.bfloat16


def bf(x):
    return np.asarray(x, np.float32).astype(BF16)


def f64(x):
    return np.asarray(x).astype(np.float64)


E2M1 = np.array([0.0, 0.5, 1.0, 1.5, 2.0, 3.0, 4.0, 6.0, -0.0, -0.5, -1.0, -1.5, -2.0, -3.0, -4.0, -6.0])


def pack_weight(w, fmt):
    k, n = w.shape
    w = f64(bf(w)).reshape(k // 32, 32, n)
    amax = np.abs(w).max(1)
    if fmt == "e4m3":
        byte = np.frexp(amax)[1] - 1 + 127 - 7
    else:
        mant, ex = np.frexp(amax / 6.0)
        byte = np.where(mant > 0.5, ex, ex - 1) + 127
    byte = np.clip(np.where(amax > 0, byte, 1), 1, 254)
    scaled = (w * np.exp2(127.0 - byte)[:, None, :]).reshape(k, n).astype(np.float32)
    by_word = np.ascontiguousarray(scaled.reshape(k // 512, 128, 4, n).transpose(0, 1, 3, 2))
    if fmt == "e4m3":
        words = by_word.astype(ml_dtypes.float8_e4m3fn).view(np.uint8)
    else:
        c = by_word.astype(ml_dtypes.float4_e2m1fn).view(np.uint8) & 0xF
        words = c[..., 0::2] | (c[..., 1::2] << 4)
    return np.ascontiguousarray(words), np.ascontiguousarray(byte.astype(np.uint8).reshape(k // 512, 16, n))


def unpack_weight(words, scales, fmt):
    g, p, n, _ = words.shape
    if fmt == "e4m3":
        vals = np.ascontiguousarray(words).view(ml_dtypes.float8_e4m3fn).astype(np.float64)
    else:
        nib = np.empty((g, p, n, 4), np.uint8)
        nib[..., 0::2] = words & 0xF
        nib[..., 1::2] = words >> 4
        vals = E2M1[nib]
    vals = vals * np.repeat(np.exp2(scales.astype(np.float64) - 127.0), 8, axis=1)[..., None]
    return vals.transpose(0, 1, 3, 2).reshape(g * 512, n)


B, NH, T, D, N, CK = 1, 6, 1024, 512, 256, 512
THETA = 2.0 ** 16


def get_freqs(n):
    q = f64(np.repeat(np.arange(0, n, 2), 2))
    return 1.0 / (THETA ** (q / n)) / (2.0 * np.pi)


def rope(phases, v):
    ph = phases * (2.0 * np.pi)
    c, s = np.cos(ph), np.sin(ph)
    even = v[..., 0::2]
    odd = v[..., 1::2]
    v_rot = np.stack((-odd, even), axis=-1).reshape(v.shape)
    return v * c + v_rot * s


def setup_inputs():
    s = mx_kscale(D)
    x = bf(np.random.standard_normal((B, 1, T, D)) * s)
    stack = np.random.standard_normal((NH, D, N)) * 0.5 / np.sqrt(D) / s[:, None]
    words, scales = pack_weight(stack.reshape(-1, N), 'e4m3')
    return {'x': x, 'encoder_words': words, 'encoder_scales': scales}


def reference(x, encoder_words, encoder_scales):
    enc = unpack_weight(encoder_words, encoder_scales, 'e4m3').reshape(NH, D, N)
    x_latent = mxq(f64(x), 3, 'e4m3') @ enc
    x_sparse = np.maximum(x_latent, 0.0)
    phases = f64(np.arange(T))[:, None] * get_freqs(N)[None, :]
    qr = rope(phases, x_sparse)
    return x_sparse, qr

@@ -1,0 +1,220 @@
+import math
+from contextlib import ExitStack
+
+import concourse.mybir as mybir
+from concourse.masks import make_identity
+
+F32 = mybir.dt.float32
+BF16 = mybir.dt.bfloat16
+I32 = mybir.dt.int32
+U32 = mybir.dt.uint32
+U8 = mybir.dt.uint8
+FP8X4 = mybir.dt.float8_e4m3fn_x4
+ALU = mybir.AluOpType
+ACT = mybir.ActivationFunctionType
+
+P = 128
+T = 1024
+D = 512
+HEADS = 6
+N = 256
+PAIRS = N // 2
+J = T // P
+HALF_J = J // 2
+BANK_J = 2
+BANK = BANK_J * N
+CHUNK = HALF_J * N
+BANKS = HALF_J // BANK_J
+WORDS = D // 2
+OCTAVE = 8
+ROUND_MAGIC = 1.5 * 2.0**23
+PREPARE_HALF_1_BEFORE_CHUNK = 2
+
+FLOPS = 2 * T * D * HEADS * N
+
+
+def tile_bdhlayer_pa_e_kernel(tc, x, encoder_words, encoder_scales, out_0, out_1):
+    nc = tc.nc
+    with ExitStack() as ctx:
+        ctx.enter_context(tc.manual_schedule())
+        keep = ctx.enter_context(tc.tile_pool(name="keep", bufs=1))
+        work = ctx.enter_context(tc.tile_pool(name="work", bufs=3))
+        psum_t = ctx.enter_context(tc.psum_pool(name="psum_t", bufs=2))
+        psum_acc = ctx.enter_context(tc.psum_pool(name="psum_acc", bufs=6))
+
+        x_rows = x[0, 0].rearrange("(p j) k -> p j k", j=J)
+        x_sb = keep.tile([P, J, D], BF16)
+        w_words = keep.tile([P, HEADS, N], U32, align_bytes=64)
+        w_scales = keep.tile([P, HEADS, N], U8, align_bytes=64)
+
+        nc.vector.memset(w_scales[:].rearrange("p h n -> p (h n)").bitcast(I32), 0)
+
+        nc.sync.dma_start(out=x_sb[:, 0:HALF_J, :], in_=x_rows[:, 0:HALF_J, :])
+        nc.sync.dma_start(
+            out=w_words[:].bitcast(I32),
+            in_=encoder_words.rearrange("h p n t -> p h (n t)").bitcast(I32),
+        )
+        for quadrant in range(4):
+            nc.sync.dma_start(
+                out=w_scales[32 * quadrant : 32 * quadrant + 4, :, :].bitcast(I32),
+                in_=encoder_scales[:, 4 * quadrant : 4 * quadrant + 4, :].rearrange("h r n -> r h n").bitcast(I32),
+            )
+        nc.sync.dma_start(out=x_sb[:, HALF_J:J, :], in_=x_rows[:, HALF_J:J, :])
+
+        token_int = keep.tile([P, J], I32)
+        nc.gpsimd.iota(token_int[:], pattern=[[1, J]], base=0, channel_multiplier=J)
+        identity = keep.tile([P, P], F32)
+        make_identity(nc, identity[:])
+
+        one = keep.tile([P, 1], F32)
+        nc.vector.memset(one[:], 1.0)
+        turns = keep.tile([P, PAIRS], F32)
+        for i in range(OCTAVE):
+            nc.vector.tensor_scalar_mul(
+                out=turns[:, i : i + 1], in0=one[:], scalar1=2.0 ** (-i / OCTAVE) / (2.0 * math.pi)
+            )
+        done = OCTAVE
+        while done < PAIRS:
+            nc.vector.tensor_scalar_mul(
+                out=turns[:, done : 2 * done], in0=turns[:, 0:done], scalar1=2.0 ** (-done // OCTAVE)
+            )
+            done *= 2
+        token = keep.tile([P, J], F32)
+        nc.vector.tensor_copy(out=token[:], in_=token_int[:])
+
+        def make_tables(half):
+            shape = [P, HALF_J, PAIRS]
+            j_range = slice(half * HALF_J, (half + 1) * HALF_J)
+            phase = keep.tile(shape, F32, name="phase")
+            nc.vector.tensor_tensor(
+                out=phase[:],
+                in0=token[:, j_range].unsqueeze(2).to_broadcast(shape),
+                in1=turns[:].unsqueeze(1).to_broadcast(shape),
+                op=ALU.mult,
+            )
+            whole = keep.tile(shape, F32, name="whole")
+            nc.vector.tensor_scalar(
+                out=whole[:], in0=phase[:], scalar1=ROUND_MAGIC, scalar2=ROUND_MAGIC, op0=ALU.add, op1=ALU.subtract
+            )
+            frac = keep.tile(shape, F32, name="frac")
+            nc.vector.tensor_tensor(out=frac[:], in0=phase[:], in1=whole[:], op=ALU.subtract)
+            minus_abs = keep.tile(shape, F32, name="minus_abs")
+            nc.vector.scalar_tensor_tensor(
+                out=minus_abs[:], in0=frac[:], scalar=-1.0, in1=frac[:], op0=ALU.mult, op1=ALU.min
+            )
+            quarter_less = keep.tile(shape, F32, name="quarter_less")
+            nc.vector.tensor_scalar_add(out=quarter_less[:], in0=minus_abs[:], scalar1=0.25)
+
+            sin = keep.tile(shape, F32, name="sin%d" % half)
+            minus_sin = keep.tile(shape, F32, name="minus_sin%d" % half)
+            cos = keep.tile(shape, F32, name="cos%d" % half)
+            nc.scalar.activation(out=sin[:], in_=frac[:], func=ACT.Sin, scale=2.0 * math.pi)
+            nc.scalar.activation(out=minus_sin[:], in_=frac[:], func=ACT.Sin, scale=-2.0 * math.pi)
+            nc.scalar.activation(out=cos[:], in_=quarter_less[:], func=ACT.Sin, scale=2.0 * math.pi)
+            return cos, sin, minus_sin
+
+        def quantise_x(half):
+            x_words = x_sb[:].rearrange("p j k -> p (j k)").bitcast(F32)
+            grouped = keep.tile([P, HALF_J, P, 4], BF16, name="grouped%d" % half, align_bytes=64)
+            grouped_words = grouped[:].rearrange("q j t e -> q (j t e)").bitcast(F32).rearrange(
+                "q (j t u) -> q j t u", j=HALF_J, u=2
+            )
+            for b in range(BANKS):
+                flipped = psum_t.tile([P, BANK_J, 2, P], F32, name="flipped")
+                for jj in range(BANK_J):
+                    first = (half * HALF_J + b * BANK_J + jj) * WORDS
+                    for u in range(2):
+                        nc.tensor.transpose(
+                            out=flipped[:, jj, u, :],
+                            in_=x_words[:, first + u : first + WORDS : 2],
+                            identity=identity[:],
+                        )
+                copy = nc.vector.tensor_copy if b % 2 == 0 else nc.scalar.copy
+                copy(
+                    out=grouped_words[:, b * BANK_J : (b + 1) * BANK_J, :, :],
+                    in_=flipped[:].rearrange("q j u t -> q j t u"),
+                )
+            codes = keep.tile([P, HALF_J * P], U32, name="codes%d" % half, align_bytes=64)
+            scales = keep.tile([P, HALF_J * P], U8, name="scales%d" % half, align_bytes=64)
+            nc.vector.quantize_mx(
+                out=codes[:].bitcast(FP8X4),
+                scales=scales[:],
+                in_=grouped[:].rearrange("q j t e -> q (j t e)"),
+            )
+            return codes, scales
+
+        def prepare(half):
+            return make_tables(half) + quantise_x(half)
+
+        sparse_rows = out_0[0].rearrange("h (p j) n -> h p j n", j=J)
+        rotated_rows = out_1[0].rearrange("h (p j) n -> h p j n", j=J)
+        prepared = {0: prepare(0)}
+
+        for chunk in range(2 * HEADS):
+            if chunk == PREPARE_HALF_1_BEFORE_CHUNK:
+                prepared[1] = prepare(1)
+            half, head = divmod(chunk, HEADS)
+            cos, sin, minus_sin, codes, scales = prepared[half]
+            j_range = slice(half * HALF_J, (half + 1) * HALF_J)
+
+            sparse = work.tile([P, CHUNK], F32, name="sparse")
+            with_cos = work.tile([P, CHUNK], F32, name="with_cos")
+            with_sin = work.tile([P, 2, CHUNK // 2], F32, name="with_sin")
+            rotated = work.tile([P, CHUNK], F32, name="rotated")
+
+            for b in range(BANKS):
+                latent = psum_acc.tile([P, BANK], F32, name="latent")
+                for jj in range(BANK_J):
+                    tokens = slice((b * BANK_J + jj) * P, (b * BANK_J + jj + 1) * P)
+                    nc.tensor.matmul_mx(
+                        out=latent[:, jj * N : (jj + 1) * N],
+                        lhsT=codes[:, tokens].bitcast(FP8X4),
+                        lhsT_scale=scales[:, tokens],
+                        rhs=w_words[:, head, :].bitcast(FP8X4),
+                        rhs_scale=w_scales[:, head, :],
+                        start=True,
+                        stop=True,
+                    )
+                columns = slice(b * BANK, (b + 1) * BANK)
+                pairs = slice(b * BANK // 2, (b + 1) * BANK // 2)
+                bank_j = slice(b * BANK_J, (b + 1) * BANK_J)
+                nc.scalar.activation(out=sparse[:, columns], in_=latent[:], func=ACT.Relu)
+
+                latent_pairs = latent[:].rearrange("p (q c) -> p q c", c=2)
+                nc.vector.scalar_tensor_tensor(
+                    out=with_cos[:, columns].rearrange("p (q c) -> p q c", c=2),
+                    in0=latent_pairs,
+                    scalar=0.0,
+                    in1=cos[:, bank_j, :].rearrange("p j i -> p (j i)").unsqueeze(2).to_broadcast([P, BANK // 2, 2]),
+                    op0=ALU.max,
+                    op1=ALU.mult,
+                )
+                nc.vector.scalar_tensor_tensor(
+                    out=with_sin[:, 0, pairs],
+                    in0=latent_pairs[:, :, 1],
+                    scalar=0.0,
+                    in1=minus_sin[:, bank_j, :].rearrange("p j i -> p (j i)"),
+                    op0=ALU.max,
+                    op1=ALU.mult,
+                )
+                nc.vector.scalar_tensor_tensor(
+                    out=with_sin[:, 1, pairs],
+                    in0=latent_pairs[:, :, 0],
+                    scalar=0.0,
+                    in1=sin[:, bank_j, :].rearrange("p j i -> p (j i)"),
+                    op0=ALU.max,
+                    op1=ALU.mult,
+                )
+
+            nc.scalar.dma_start(
+                out=sparse_rows[head][:, j_range, :], in_=sparse[:].rearrange("p (j n) -> p j n", n=N)
+            )
+            nc.gpsimd.tensor_tensor(
+                out=rotated[:].rearrange("p (q c) -> p q c", c=2),
+                in0=with_cos[:].rearrange("p (q c) -> p q c", c=2),
+                in1=with_sin[:].rearrange("p c q -> p q c"),
+                op=ALU.add,
+            )
+            nc.sync.dma_start(
+                out=rotated_rows[head][:, j_range, :], in_=rotated[:].rearrange("p (j n) -> p j n", n=N)
+            )

@@ -28,7 +28,7 @@ BANKS = HALF_J // BANK_J
 WORDS = D // 2
 OCTAVE = 8
 ROUND_MAGIC = 1.5 * 2.0**23
-PREPARE_HALF_1_BEFORE_CHUNK = 2
+VECTOR_ADDS = N
 
 FLOPS = 2 * T * D * HEADS * N
 
@@ -38,7 +38,7 @@ def tile_bdhlayer_pa_e_kernel(tc, x, encoder_words, encoder_scales, out_0, out_1
     with ExitStack() as ctx:
         ctx.enter_context(tc.manual_schedule())
         keep = ctx.enter_context(tc.tile_pool(name="keep", bufs=1))
-        work = ctx.enter_context(tc.tile_pool(name="work", bufs=3))
+        work = ctx.enter_context(tc.tile_pool(name="work", bufs=4))
         psum_t = ctx.enter_context(tc.psum_pool(name="psum_t", bufs=2))
         psum_acc = ctx.enter_context(tc.psum_pool(name="psum_acc", bufs=6))
 
@@ -49,7 +49,12 @@ def tile_bdhlayer_pa_e_kernel(tc, x, encoder_words, encoder_scales, out_0, out_1
 
         nc.vector.memset(w_scales[:].rearrange("p h n -> p (h n)").bitcast(I32), 0)
 
-        nc.sync.dma_start(out=x_sb[:, 0:HALF_J, :], in_=x_rows[:, 0:HALF_J, :])
+        def load_x(half):
+            for b in range(BANKS):
+                bank_j = slice(half * HALF_J + b * BANK_J, half * HALF_J + (b + 1) * BANK_J)
+                nc.sync.dma_start(out=x_sb[:, bank_j, :], in_=x_rows[:, bank_j, :])
+
+        load_x(0)
         nc.sync.dma_start(
             out=w_words[:].bitcast(I32),
             in_=encoder_words.rearrange("h p n t -> p h (n t)").bitcast(I32),
@@ -59,7 +64,7 @@ def tile_bdhlayer_pa_e_kernel(tc, x, encoder_words, encoder_scales, out_0, out_1
                 out=w_scales[32 * quadrant : 32 * quadrant + 4, :, :].bitcast(I32),
                 in_=encoder_scales[:, 4 * quadrant : 4 * quadrant + 4, :].rearrange("h r n -> r h n").bitcast(I32),
             )
-        nc.sync.dma_start(out=x_sb[:, HALF_J:J, :], in_=x_rows[:, HALF_J:J, :])
+        load_x(1)
 
         token_int = keep.tile([P, J], I32)
         nc.gpsimd.iota(token_int[:], pattern=[[1, J]], base=0, channel_multiplier=J)
@@ -82,43 +87,48 @@ def tile_bdhlayer_pa_e_kernel(tc, x, encoder_words, encoder_scales, out_0, out_1
         token = keep.tile([P, J], F32)
         nc.vector.tensor_copy(out=token[:], in_=token_int[:])
 
-        def make_tables(half):
-            shape = [P, HALF_J, PAIRS]
+        table_shape = [P, HALF_J, PAIRS]
+        frac = {}
+        cos = {}
+        sines = {}
+        grouped = {}
+        codes = {}
+        scales = {}
+
+        def make_angles(half):
             j_range = slice(half * HALF_J, (half + 1) * HALF_J)
-            phase = keep.tile(shape, F32, name="phase")
+            phase = keep.tile(table_shape, F32, name="phase")
             nc.vector.tensor_tensor(
                 out=phase[:],
-                in0=token[:, j_range].unsqueeze(2).to_broadcast(shape),
-                in1=turns[:].unsqueeze(1).to_broadcast(shape),
+                in0=token[:, j_range].unsqueeze(2).to_broadcast(table_shape),
+                in1=turns[:].unsqueeze(1).to_broadcast(table_shape),
                 op=ALU.mult,
             )
-            whole = keep.tile(shape, F32, name="whole")
+            whole = keep.tile(table_shape, F32, name="whole")
             nc.vector.tensor_scalar(
                 out=whole[:], in0=phase[:], scalar1=ROUND_MAGIC, scalar2=ROUND_MAGIC, op0=ALU.add, op1=ALU.subtract
             )
-            frac = keep.tile(shape, F32, name="frac")
-            nc.vector.tensor_tensor(out=frac[:], in0=phase[:], in1=whole[:], op=ALU.subtract)
-            minus_abs = keep.tile(shape, F32, name="minus_abs")
-            nc.vector.scalar_tensor_tensor(
-                out=minus_abs[:], in0=frac[:], scalar=-1.0, in1=frac[:], op0=ALU.mult, op1=ALU.min
-            )
-            quarter_less = keep.tile(shape, F32, name="quarter_less")
-            nc.vector.tensor_scalar_add(out=quarter_less[:], in0=minus_abs[:], scalar1=0.25)
+            frac[half] = keep.tile(table_shape, F32, name="frac%d" % half)
+            nc.vector.tensor_tensor(out=frac[half][:], in0=phase[:], in1=whole[:], op=ALU.subtract)
 
-            sin = keep.tile(shape, F32, name="sin%d" % half)
-            minus_sin = keep.tile(shape, F32, name="minus_sin%d" % half)
-            cos = keep.tile(shape, F32, name="cos%d" % half)
-            nc.scalar.activation(out=sin[:], in_=frac[:], func=ACT.Sin, scale=2.0 * math.pi)
-            nc.scalar.activation(out=minus_sin[:], in_=frac[:], func=ACT.Sin, scale=-2.0 * math.pi)
-            nc.scalar.activation(out=cos[:], in_=quarter_less[:], func=ACT.Sin, scale=2.0 * math.pi)
-            return cos, sin, minus_sin
+        def make_tables(half):
+            half_sin = keep.tile(table_shape, F32, name="half_sin")
+            nc.scalar.activation(out=half_sin[:], in_=frac[half][:], func=ACT.Sin, scale=math.pi)
+            twice_square = keep.tile(table_shape, F32, name="twice_square")
+            nc.scalar.activation(out=twice_square[:], in_=half_sin[:], func=ACT.Square, scale=math.sqrt(2.0))
+            cos[half] = keep.tile(table_shape, F32, name="cos%d" % half)
+            nc.scalar.activation(out=cos[half][:], in_=twice_square[:], func=ACT.Copy, scale=-1.0, bias=1.0)
+            sines[half] = keep.tile([P, 2, HALF_J, PAIRS], F32, name="sines%d" % half)
+            nc.scalar.activation(out=sines[half][:, 0, :, :], in_=frac[half][:], func=ACT.Sin, scale=-2.0 * math.pi)
+            nc.scalar.activation(out=sines[half][:, 1, :, :], in_=frac[half][:], func=ACT.Sin, scale=2.0 * math.pi)
 
-        def quantise_x(half):
+        def flip_x(half):
             x_words = x_sb[:].rearrange("p j k -> p (j k)").bitcast(F32)
-            grouped = keep.tile([P, HALF_J, P, 4], BF16, name="grouped%d" % half, align_bytes=64)
-            grouped_words = grouped[:].rearrange("q j t e -> q (j t e)").bitcast(F32).rearrange(
+            grouped[half] = keep.tile([P, HALF_J, P, 4], BF16, name="grouped%d" % half, align_bytes=64)
+            grouped_words = grouped[half][:].rearrange("q j t e -> q (j t e)").bitcast(F32).rearrange(
                 "q (j t u) -> q j t u", j=HALF_J, u=2
             )
+            copy = nc.vector.tensor_copy if half == 0 else nc.scalar.copy
             for b in range(BANKS):
                 flipped = psum_t.tile([P, BANK_J, 2, P], F32, name="flipped")
                 for jj in range(BANK_J):
@@ -129,37 +139,38 @@ def tile_bdhlayer_pa_e_kernel(tc, x, encoder_words, encoder_scales, out_0, out_1
                             in_=x_words[:, first + u : first + WORDS : 2],
                             identity=identity[:],
                         )
-                copy = nc.vector.tensor_copy if b % 2 == 0 else nc.scalar.copy
                 copy(
                     out=grouped_words[:, b * BANK_J : (b + 1) * BANK_J, :, :],
                     in_=flipped[:].rearrange("q j u t -> q j t u"),
                 )
-            codes = keep.tile([P, HALF_J * P], U32, name="codes%d" % half, align_bytes=64)
-            scales = keep.tile([P, HALF_J * P], U8, name="scales%d" % half, align_bytes=64)
-            nc.vector.quantize_mx(
-                out=codes[:].bitcast(FP8X4),
-                scales=scales[:],
-                in_=grouped[:].rearrange("q j t e -> q (j t e)"),
-            )
-            return codes, scales
 
-        def prepare(half):
-            return make_tables(half) + quantise_x(half)
+        def quantise_x(half):
+            codes[half] = keep.tile([P, HALF_J * P], U32, name="codes%d" % half, align_bytes=64)
+            scales[half] = keep.tile([P, HALF_J * P], U8, name="scales%d" % half, align_bytes=64)
+            for b in range(BANKS):
+                tokens = slice(b * BANK_J * P, (b + 1) * BANK_J * P)
+                nc.vector.quantize_mx(
+                    out=codes[half][:, tokens].bitcast(FP8X4),
+                    scales=scales[half][:, tokens],
+                    in_=grouped[half][:, b * BANK_J : (b + 1) * BANK_J, :, :].rearrange("q j t e -> q (j t e)"),
+                )
+
+        preparation = (make_angles, make_tables, flip_x, quantise_x)
 
         sparse_rows = out_0[0].rearrange("h (p j) n -> h p j n", j=J)
         rotated_rows = out_1[0].rearrange("h (p j) n -> h p j n", j=J)
-        prepared = {0: prepare(0)}
+        for step in preparation:
+            step(0)
 
         for chunk in range(2 * HEADS):
-            if chunk == PREPARE_HALF_1_BEFORE_CHUNK:
-                prepared[1] = prepare(1)
+            if 1 <= chunk <= len(preparation):
+                preparation[chunk - 1](1)
             half, head = divmod(chunk, HEADS)
-            cos, sin, minus_sin, codes, scales = prepared[half]
             j_range = slice(half * HALF_J, (half + 1) * HALF_J)
 
             sparse = work.tile([P, CHUNK], F32, name="sparse")
             with_cos = work.tile([P, CHUNK], F32, name="with_cos")
-            with_sin = work.tile([P, 2, CHUNK // 2], F32, name="with_sin")
+            with_sin = work.tile([P, CHUNK], F32, name="with_sin")
             rotated = work.tile([P, CHUNK], F32, name="rotated")
 
             for b in range(BANKS):
@@ -168,52 +179,45 @@ def tile_bdhlayer_pa_e_kernel(tc, x, encoder_words, encoder_scales, out_0, out_1
                     tokens = slice((b * BANK_J + jj) * P, (b * BANK_J + jj + 1) * P)
                     nc.tensor.matmul_mx(
                         out=latent[:, jj * N : (jj + 1) * N],
-                        lhsT=codes[:, tokens].bitcast(FP8X4),
-                        lhsT_scale=scales[:, tokens],
+                        lhsT=codes[half][:, tokens].bitcast(FP8X4),
+                        lhsT_scale=scales[half][:, tokens],
                         rhs=w_words[:, head, :].bitcast(FP8X4),
                         rhs_scale=w_scales[:, head, :],
                         start=True,
                         stop=True,
                     )
                 columns = slice(b * BANK, (b + 1) * BANK)
-                pairs = slice(b * BANK // 2, (b + 1) * BANK // 2)
                 bank_j = slice(b * BANK_J, (b + 1) * BANK_J)
-                nc.scalar.activation(out=sparse[:, columns], in_=latent[:], func=ACT.Relu)
-
                 latent_pairs = latent[:].rearrange("p (q c) -> p q c", c=2)
                 nc.vector.scalar_tensor_tensor(
                     out=with_cos[:, columns].rearrange("p (q c) -> p q c", c=2),
                     in0=latent_pairs,
                     scalar=0.0,
-                    in1=cos[:, bank_j, :].rearrange("p j i -> p (j i)").unsqueeze(2).to_broadcast([P, BANK // 2, 2]),
+                    in1=cos[half][:, bank_j, :].rearrange("p j i -> p (j i)").unsqueeze(2).to_broadcast([P, BANK // 2, 2]),
                     op0=ALU.max,
                     op1=ALU.mult,
                 )
                 nc.vector.scalar_tensor_tensor(
-                    out=with_sin[:, 0, pairs],
-                    in0=latent_pairs[:, :, 1],
+                    out=with_sin[:, columns].rearrange("p (q c) -> p q c", c=2),
+                    in0=latent_pairs[:, :, ::-1],
                     scalar=0.0,
-                    in1=minus_sin[:, bank_j, :].rearrange("p j i -> p (j i)"),
+                    in1=sines[half][:, :, bank_j, :].rearrange("p c j i -> p (j i) c"),
                     op0=ALU.max,
                     op1=ALU.mult,
                 )
-                nc.vector.scalar_tensor_tensor(
-                    out=with_sin[:, 1, pairs],
-                    in0=latent_pairs[:, :, 0],
-                    scalar=0.0,
-                    in1=sin[:, bank_j, :].rearrange("p j i -> p (j i)"),
-                    op0=ALU.max,
-                    op1=ALU.mult,
+                nc.scalar.activation(out=sparse[:, columns], in_=latent[:], func=ACT.Relu)
+
+                gpsimd_adds = slice(max(b * BANK, VECTOR_ADDS), (b + 1) * BANK)
+                nc.gpsimd.tensor_tensor(
+                    out=rotated[:, gpsimd_adds], in0=with_cos[:, gpsimd_adds], in1=with_sin[:, gpsimd_adds], op=ALU.add
                 )
+            vector_adds = slice(0, VECTOR_ADDS)
+            nc.vector.tensor_tensor(
+                out=rotated[:, vector_adds], in0=with_cos[:, vector_adds], in1=with_sin[:, vector_adds], op=ALU.add
+            )
 
             nc.scalar.dma_start(
                 out=sparse_rows[head][:, j_range, :], in_=sparse[:].rearrange("p (j n) -> p j n", n=N)
-            )
-            nc.gpsimd.tensor_tensor(
-                out=rotated[:].rearrange("p (q c) -> p q c", c=2),
-                in0=with_cos[:].rearrange("p (q c) -> p q c", c=2),
-                in1=with_sin[:].rearrange("p c q -> p q c"),
-                op=ALU.add,
             )
             nc.sync.dma_start(
                 out=rotated_rows[head][:, j_range, :], in_=rotated[:].rearrange("p (j n) -> p j n", n=N)

@@ -36,7 +36,6 @@ FLOPS = 2 * T * D * HEADS * N
 def tile_bdhlayer_pa_e_kernel(tc, x, encoder_words, encoder_scales, out_0, out_1):
     nc = tc.nc
     with ExitStack() as ctx:
-        ctx.enter_context(tc.manual_schedule())
         keep = ctx.enter_context(tc.tile_pool(name="keep", bufs=1))
         work = ctx.enter_context(tc.tile_pool(name="work", bufs=4))
         psum_t = ctx.enter_context(tc.psum_pool(name="psum_t", bufs=2))

@@ -28,7 +28,6 @@ BANKS = HALF_J // BANK_J
 WORDS = D // 2
 OCTAVE = 8
 ROUND_MAGIC = 1.5 * 2.0**23
-VECTOR_ADDS = N
 
 FLOPS = 2 * T * D * HEADS * N
 
@@ -206,14 +205,7 @@ def tile_bdhlayer_pa_e_kernel(tc, x, encoder_words, encoder_scales, out_0, out_1
                 )
                 nc.scalar.activation(out=sparse[:, columns], in_=latent[:], func=ACT.Relu)
 
-                gpsimd_adds = slice(max(b * BANK, VECTOR_ADDS), (b + 1) * BANK)
-                nc.gpsimd.tensor_tensor(
-                    out=rotated[:, gpsimd_adds], in0=with_cos[:, gpsimd_adds], in1=with_sin[:, gpsimd_adds], op=ALU.add
-                )
-            vector_adds = slice(0, VECTOR_ADDS)
-            nc.vector.tensor_tensor(
-                out=rotated[:, vector_adds], in0=with_cos[:, vector_adds], in1=with_sin[:, vector_adds], op=ALU.add
-            )
+            nc.gpsimd.tensor_tensor(out=rotated[:], in0=with_cos[:], in1=with_sin[:], op=ALU.add)
 
             nc.scalar.dma_start(
                 out=sparse_rows[head][:, j_range, :], in_=sparse[:].rearrange("p (j n) -> p j n", n=N)

@@ -26,6 +26,7 @@ BANK = BANK_J * N
 CHUNK = HALF_J * N
 BANKS = HALF_J // BANK_J
 WORDS = D // 2
+OCTAVES = 16
 OCTAVE = 8
 ROUND_MAGIC = 1.5 * 2.0**23
 
@@ -36,180 +37,234 @@ def tile_bdhlayer_pa_e_kernel(tc, x, encoder_words, encoder_scales, out_0, out_1
     nc = tc.nc
     with ExitStack() as ctx:
         keep = ctx.enter_context(tc.tile_pool(name="keep", bufs=1))
-        work = ctx.enter_context(tc.tile_pool(name="work", bufs=4))
+        products = ctx.enter_context(tc.tile_pool(name="products", bufs=4))
+        results = ctx.enter_context(tc.tile_pool(name="results", bufs=6))
         psum_t = ctx.enter_context(tc.psum_pool(name="psum_t", bufs=2))
         psum_acc = ctx.enter_context(tc.psum_pool(name="psum_acc", bufs=6))
+        ctx.enter_context(tc.manual_schedule())
 
         x_rows = x[0, 0].rearrange("(p j) k -> p j k", j=J)
         x_sb = keep.tile([P, J, D], BF16)
         w_words = keep.tile([P, HEADS, N], U32, align_bytes=64)
         w_scales = keep.tile([P, HEADS, N], U8, align_bytes=64)
 
-        nc.vector.memset(w_scales[:].rearrange("p h n -> p (h n)").bitcast(I32), 0)
+        one = keep.tile([P, 1], F32)
+        nc.vector.memset(one[:], 1.0)
+        warm = keep.tile([P, 1], F32)
+        nc.scalar.activation(out=warm[:], in_=one[:], func=ACT.Sin)
 
-        def load_x(half):
-            for b in range(BANKS):
-                bank_j = slice(half * HALF_J + b * BANK_J, half * HALF_J + (b + 1) * BANK_J)
-                nc.sync.dma_start(out=x_sb[:, bank_j, :], in_=x_rows[:, bank_j, :])
+        nc.gpsimd.memset(w_scales[:].rearrange("p h n -> p (h n)").bitcast(F32), 0.0)
+
+        def load_x(pair):
+            pair_j = slice(pair * BANK_J, (pair + 1) * BANK_J)
+            nc.sync.dma_start(out=x_sb[:, pair_j, :], in_=x_rows[:, pair_j, :])
+
+        def load_words(first, last):
+            nc.sync.dma_start(
+                out=w_words[:, first:last, :].bitcast(I32),
+                in_=encoder_words[first:last].rearrange("h p n t -> p h (n t)").bitcast(I32),
+            )
 
         load_x(0)
-        nc.sync.dma_start(
-            out=w_words[:].bitcast(I32),
-            in_=encoder_words.rearrange("h p n t -> p h (n t)").bitcast(I32),
-        )
+        load_x(1)
         for quadrant in range(4):
             nc.sync.dma_start(
                 out=w_scales[32 * quadrant : 32 * quadrant + 4, :, :].bitcast(I32),
                 in_=encoder_scales[:, 4 * quadrant : 4 * quadrant + 4, :].rearrange("h r n -> r h n").bitcast(I32),
             )
-        load_x(1)
+        load_words(0, 1)
+        load_x(2)
+        load_x(3)
+        load_words(1, HEADS)
 
         token_int = keep.tile([P, J], I32)
         nc.gpsimd.iota(token_int[:], pattern=[[1, J]], base=0, channel_multiplier=J)
+        exponent = keep.tile([P, OCTAVES], I32)
+        nc.gpsimd.iota(exponent[:], pattern=[[-1, OCTAVES]], base=127, channel_multiplier=0)
         identity = keep.tile([P, P], F32)
         make_identity(nc, identity[:])
 
-        one = keep.tile([P, 1], F32)
-        nc.vector.memset(one[:], 1.0)
-        turns = keep.tile([P, PAIRS], F32)
-        for i in range(OCTAVE):
+        octave = keep.tile([P, OCTAVE], F32)
+        for r in range(OCTAVE):
             nc.vector.tensor_scalar_mul(
-                out=turns[:, i : i + 1], in0=one[:], scalar1=2.0 ** (-i / OCTAVE) / (2.0 * math.pi)
+                out=octave[:, r : r + 1], in0=one[:], scalar1=2.0 ** (-r / OCTAVE) / (2.0 * math.pi)
             )
-        done = OCTAVE
-        while done < PAIRS:
-            nc.vector.tensor_scalar_mul(
-                out=turns[:, done : 2 * done], in0=turns[:, 0:done], scalar1=2.0 ** (-done // OCTAVE)
-            )
-            done *= 2
+        halvings = keep.tile([P, OCTAVES], I32)
+        nc.vector.tensor_single_scalar(out=halvings[:], in_=exponent[:], scalar=23, op=ALU.logical_shift_left)
+        turns = keep.tile([P, OCTAVES, OCTAVE], F32)
+        nc.vector.tensor_tensor(
+            out=turns[:],
+            in0=halvings[:].bitcast(F32).unsqueeze(2).to_broadcast([P, OCTAVES, OCTAVE]),
+            in1=octave[:].unsqueeze(1).to_broadcast([P, OCTAVES, OCTAVE]),
+            op=ALU.mult,
+        )
         token = keep.tile([P, J], F32)
         nc.vector.tensor_copy(out=token[:], in_=token_int[:])
 
-        table_shape = [P, HALF_J, PAIRS]
-        frac = {}
-        cos = {}
-        sines = {}
-        grouped = {}
-        codes = {}
-        scales = {}
+        table_shape = [P, J, PAIRS]
+        phase = keep.tile(table_shape, F32)
+        whole = keep.tile(table_shape, F32)
+        frac = keep.tile(table_shape, F32)
+        half_sin = keep.tile(table_shape, F32)
+        twice_square = keep.tile(table_shape, F32)
+        cos = keep.tile(table_shape, F32)
+        sines = keep.tile([P, 2, J, PAIRS], F32)
+        grouped = keep.tile([P, J, P, 4], BF16, align_bytes=64)
+        codes = keep.tile([P, J * P], U32, align_bytes=64)
+        scales = keep.tile([P, J * P], U8, align_bytes=64)
 
-        def make_angles(half):
-            j_range = slice(half * HALF_J, (half + 1) * HALF_J)
-            phase = keep.tile(table_shape, F32, name="phase")
-            nc.vector.tensor_tensor(
-                out=phase[:],
-                in0=token[:, j_range].unsqueeze(2).to_broadcast(table_shape),
-                in1=turns[:].unsqueeze(1).to_broadcast(table_shape),
+        def make_phase(engine, js):
+            shape = [P, js.stop - js.start, PAIRS]
+            engine.tensor_tensor(
+                out=phase[:, js, :],
+                in0=token[:, js].unsqueeze(2).to_broadcast(shape),
+                in1=turns[:].rearrange("p o r -> p (o r)").unsqueeze(1).to_broadcast(shape),
                 op=ALU.mult,
             )
-            whole = keep.tile(table_shape, F32, name="whole")
+
+        def make_whole(js):
             nc.vector.tensor_scalar(
-                out=whole[:], in0=phase[:], scalar1=ROUND_MAGIC, scalar2=ROUND_MAGIC, op0=ALU.add, op1=ALU.subtract
+                out=whole[:, js, :], in0=phase[:, js, :], scalar1=ROUND_MAGIC, scalar2=ROUND_MAGIC, op0=ALU.add, op1=ALU.subtract
             )
-            frac[half] = keep.tile(table_shape, F32, name="frac%d" % half)
-            nc.vector.tensor_tensor(out=frac[half][:], in0=phase[:], in1=whole[:], op=ALU.subtract)
 
-        def make_tables(half):
-            half_sin = keep.tile(table_shape, F32, name="half_sin")
-            nc.scalar.activation(out=half_sin[:], in_=frac[half][:], func=ACT.Sin, scale=math.pi)
-            twice_square = keep.tile(table_shape, F32, name="twice_square")
-            nc.scalar.activation(out=twice_square[:], in_=half_sin[:], func=ACT.Square, scale=math.sqrt(2.0))
-            cos[half] = keep.tile(table_shape, F32, name="cos%d" % half)
-            nc.scalar.activation(out=cos[half][:], in_=twice_square[:], func=ACT.Copy, scale=-1.0, bias=1.0)
-            sines[half] = keep.tile([P, 2, HALF_J, PAIRS], F32, name="sines%d" % half)
-            nc.scalar.activation(out=sines[half][:, 0, :, :], in_=frac[half][:], func=ACT.Sin, scale=-2.0 * math.pi)
-            nc.scalar.activation(out=sines[half][:, 1, :, :], in_=frac[half][:], func=ACT.Sin, scale=2.0 * math.pi)
+        def make_frac(engine, js):
+            engine.tensor_tensor(out=frac[:, js, :], in0=phase[:, js, :], in1=whole[:, js, :], op=ALU.subtract)
 
-        def flip_x(half):
-            x_words = x_sb[:].rearrange("p j k -> p (j k)").bitcast(F32)
-            grouped[half] = keep.tile([P, HALF_J, P, 4], BF16, name="grouped%d" % half, align_bytes=64)
-            grouped_words = grouped[half][:].rearrange("q j t e -> q (j t e)").bitcast(F32).rearrange(
-                "q (j t u) -> q j t u", j=HALF_J, u=2
+        def table_steps(js):
+            return (
+                lambda: nc.scalar.activation(out=half_sin[:, js, :], in_=frac[:, js, :], func=ACT.Sin, scale=math.pi),
+                lambda: nc.scalar.activation(out=sines[:, 0, js, :], in_=frac[:, js, :], func=ACT.Sin, scale=-2.0 * math.pi),
+                lambda: nc.scalar.activation(
+                    out=twice_square[:, js, :], in_=half_sin[:, js, :], func=ACT.Square, scale=math.sqrt(2.0)
+                ),
+                lambda: nc.scalar.activation(out=sines[:, 1, js, :], in_=frac[:, js, :], func=ACT.Sin, scale=2.0 * math.pi),
+                lambda: nc.scalar.activation(out=cos[:, js, :], in_=twice_square[:, js, :], func=ACT.Copy, scale=-1.0, bias=1.0),
             )
-            copy = nc.vector.tensor_copy if half == 0 else nc.scalar.copy
-            for b in range(BANKS):
-                flipped = psum_t.tile([P, BANK_J, 2, P], F32, name="flipped")
-                for jj in range(BANK_J):
-                    first = (half * HALF_J + b * BANK_J + jj) * WORDS
-                    for u in range(2):
-                        nc.tensor.transpose(
-                            out=flipped[:, jj, u, :],
-                            in_=x_words[:, first + u : first + WORDS : 2],
-                            identity=identity[:],
-                        )
-                copy(
-                    out=grouped_words[:, b * BANK_J : (b + 1) * BANK_J, :, :],
-                    in_=flipped[:].rearrange("q j u t -> q j t u"),
-                )
 
-        def quantise_x(half):
-            codes[half] = keep.tile([P, HALF_J * P], U32, name="codes%d" % half, align_bytes=64)
-            scales[half] = keep.tile([P, HALF_J * P], U8, name="scales%d" % half, align_bytes=64)
-            for b in range(BANKS):
-                tokens = slice(b * BANK_J * P, (b + 1) * BANK_J * P)
-                nc.vector.quantize_mx(
-                    out=codes[half][:, tokens].bitcast(FP8X4),
-                    scales=scales[half][:, tokens],
-                    in_=grouped[half][:, b * BANK_J : (b + 1) * BANK_J, :, :].rearrange("q j t e -> q (j t e)"),
-                )
+        x_words = x_sb[:].rearrange("p j k -> p (j k)").bitcast(F32)
+        grouped_words = grouped[:].rearrange("q j t e -> q (j t e)").bitcast(F32).rearrange("q (j t u) -> q j t u", j=J, u=2)
 
-        preparation = (make_angles, make_tables, flip_x, quantise_x)
+        def flip_x(pair, copy):
+            flipped = psum_t.tile([P, BANK_J, 2, P], F32, name="flipped")
+            for jj in range(BANK_J):
+                first = (pair * BANK_J + jj) * WORDS
+                for u in range(2):
+                    nc.tensor.transpose(
+                        out=flipped[:, jj, u, :], in_=x_words[:, first + u : first + WORDS : 2], identity=identity[:]
+                    )
+            copy(
+                out=grouped_words[:, pair * BANK_J : (pair + 1) * BANK_J, :, :],
+                in_=flipped[:].rearrange("q j u t -> q j t u"),
+            )
+
+        def quantise_x(first_pair, last_pair):
+            tokens = slice(first_pair * BANK_J * P, last_pair * BANK_J * P)
+            nc.vector.quantize_mx(
+                out=codes[:, tokens].bitcast(FP8X4),
+                scales=scales[:, tokens],
+                in_=grouped[:, first_pair * BANK_J : last_pair * BANK_J, :, :].rearrange("q j t e -> q (j t e)"),
+            )
+
+        pair_0, pair_1, half_1 = slice(0, 2), slice(2, 4), slice(HALF_J, J)
+        make_phase(nc.vector, pair_0)
+        make_whole(pair_0)
+        make_frac(nc.vector, pair_0)
+        for step in table_steps(pair_0):
+            step()
+        make_phase(nc.vector, pair_1)
+        make_phase(nc.gpsimd, half_1)
+        flip_x(0, nc.vector.tensor_copy)
+        make_whole(pair_1)
+        quantise_x(0, 1)
+        make_frac(nc.vector, pair_1)
+        flip_x(1, nc.scalar.copy)
+        make_whole(half_1)
+        make_frac(nc.gpsimd, half_1)
+        quantise_x(1, 2)
+        for step in table_steps(pair_1):
+            step()
 
         sparse_rows = out_0[0].rearrange("h (p j) n -> h p j n", j=J)
         rotated_rows = out_1[0].rearrange("h (p j) n -> h p j n", j=J)
-        for step in preparation:
-            step(0)
+        all_banks = 2 * HEADS * BANKS
+        scalar_extras = (lambda: flip_x(2, nc.scalar.copy), lambda: flip_x(3, nc.scalar.copy)) + table_steps(half_1)
+        tiles = {}
 
-        for chunk in range(2 * HEADS):
-            if 1 <= chunk <= len(preparation):
-                preparation[chunk - 1](1)
+        def add(engine, chunk, columns):
+            engine.tensor_tensor(
+                out=tiles["rotated", chunk][:, columns],
+                in0=tiles["with_cos", chunk][:, columns],
+                in1=tiles["with_sin", chunk][:, columns],
+                op=ALU.add,
+            )
+
+        def store(queue, rows, kind, chunk, first_bank, last_bank):
             half, head = divmod(chunk, HEADS)
-            j_range = slice(half * HALF_J, (half + 1) * HALF_J)
-
-            sparse = work.tile([P, CHUNK], F32, name="sparse")
-            with_cos = work.tile([P, CHUNK], F32, name="with_cos")
-            with_sin = work.tile([P, CHUNK], F32, name="with_sin")
-            rotated = work.tile([P, CHUNK], F32, name="rotated")
-
-            for b in range(BANKS):
-                latent = psum_acc.tile([P, BANK], F32, name="latent")
-                for jj in range(BANK_J):
-                    tokens = slice((b * BANK_J + jj) * P, (b * BANK_J + jj + 1) * P)
-                    nc.tensor.matmul_mx(
-                        out=latent[:, jj * N : (jj + 1) * N],
-                        lhsT=codes[half][:, tokens].bitcast(FP8X4),
-                        lhsT_scale=scales[half][:, tokens],
-                        rhs=w_words[:, head, :].bitcast(FP8X4),
-                        rhs_scale=w_scales[:, head, :],
-                        start=True,
-                        stop=True,
-                    )
-                columns = slice(b * BANK, (b + 1) * BANK)
-                bank_j = slice(b * BANK_J, (b + 1) * BANK_J)
-                latent_pairs = latent[:].rearrange("p (q c) -> p q c", c=2)
-                nc.vector.scalar_tensor_tensor(
-                    out=with_cos[:, columns].rearrange("p (q c) -> p q c", c=2),
-                    in0=latent_pairs,
-                    scalar=0.0,
-                    in1=cos[half][:, bank_j, :].rearrange("p j i -> p (j i)").unsqueeze(2).to_broadcast([P, BANK // 2, 2]),
-                    op0=ALU.max,
-                    op1=ALU.mult,
-                )
-                nc.vector.scalar_tensor_tensor(
-                    out=with_sin[:, columns].rearrange("p (q c) -> p q c", c=2),
-                    in0=latent_pairs[:, :, ::-1],
-                    scalar=0.0,
-                    in1=sines[half][:, :, bank_j, :].rearrange("p c j i -> p (j i) c"),
-                    op0=ALU.max,
-                    op1=ALU.mult,
-                )
-                nc.scalar.activation(out=sparse[:, columns], in_=latent[:], func=ACT.Relu)
-
-            nc.gpsimd.tensor_tensor(out=rotated[:], in0=with_cos[:], in1=with_sin[:], op=ALU.add)
-
-            nc.scalar.dma_start(
-                out=sparse_rows[head][:, j_range, :], in_=sparse[:].rearrange("p (j n) -> p j n", n=N)
+            nc_j = slice(half * HALF_J + first_bank * BANK_J, half * HALF_J + last_bank * BANK_J)
+            queue.dma_start(
+                out=rows[head][:, nc_j, :],
+                in_=tiles[kind, chunk][:, first_bank * BANK : last_bank * BANK].rearrange("p (j n) -> p j n", n=N),
             )
-            nc.sync.dma_start(
-                out=rotated_rows[head][:, j_range, :], in_=rotated[:].rearrange("p (j n) -> p j n", n=N)
+
+        for bank in range(all_banks):
+            chunk, b = divmod(bank, BANKS)
+            half, head = divmod(chunk, HEADS)
+            by_bank = chunk == 0 or chunk >= 2 * HEADS - 2
+            if b == 0:
+                tiles["sparse", chunk] = results.tile([P, CHUNK], F32, name="sparse")
+                tiles["with_cos", chunk] = products.tile([P, CHUNK], F32, name="with_cos")
+                tiles["with_sin", chunk] = products.tile([P, CHUNK], F32, name="with_sin")
+                tiles["rotated", chunk] = results.tile([P, CHUNK], F32, name="rotated")
+            if bank == 6:
+                quantise_x(2, 4)
+
+            latent = psum_acc.tile([P, BANK], F32, name="latent")
+            for jj in range(BANK_J):
+                j = half * HALF_J + b * BANK_J + jj
+                tokens = slice(j * P, (j + 1) * P)
+                nc.tensor.matmul_mx(
+                    out=latent[:, jj * N : (jj + 1) * N],
+                    lhsT=codes[:, tokens].bitcast(FP8X4),
+                    lhsT_scale=scales[:, tokens],
+                    rhs=w_words[:, head, :].bitcast(FP8X4),
+                    rhs_scale=w_scales[:, head, :],
+                    start=True,
+                    stop=True,
+                )
+            columns = slice(b * BANK, (b + 1) * BANK)
+            bank_j = slice(half * HALF_J + b * BANK_J, half * HALF_J + (b + 1) * BANK_J)
+            latent_pairs = latent[:].rearrange("p (q c) -> p q c", c=2)
+            nc.vector.scalar_tensor_tensor(
+                out=tiles["with_cos", chunk][:, columns].rearrange("p (q c) -> p q c", c=2),
+                in0=latent_pairs,
+                scalar=0.0,
+                in1=cos[:, bank_j, :].rearrange("p j i -> p (j i)").unsqueeze(2).to_broadcast([P, BANK // 2, 2]),
+                op0=ALU.max,
+                op1=ALU.mult,
             )
+            nc.vector.scalar_tensor_tensor(
+                out=tiles["with_sin", chunk][:, columns].rearrange("p (q c) -> p q c", c=2),
+                in0=latent_pairs[:, :, ::-1],
+                scalar=0.0,
+                in1=sines[:, :, bank_j, :].rearrange("p c j i -> p (j i) c"),
+                op0=ALU.max,
+                op1=ALU.mult,
+            )
+            nc.scalar.activation(out=tiles["sparse", chunk][:, columns], in_=latent[:], func=ACT.Relu)
+            if by_bank:
+                store(nc.scalar, sparse_rows, "sparse", chunk, b, b + 1)
+            elif b == BANKS - 1:
+                store(nc.scalar, sparse_rows, "sparse", chunk, 0, BANKS)
+            if 1 <= bank <= len(scalar_extras):
+                scalar_extras[bank - 1]()
+
+            if chunk < 2 * HEADS - 1:
+                if by_bank:
+                    add(nc.gpsimd, chunk, columns)
+                    store(nc.sync, rotated_rows, "rotated", chunk, b, b + 1)
+                elif b == BANKS - 1:
+                    add(nc.gpsimd, chunk, slice(0, CHUNK))
+                    store(nc.sync, rotated_rows, "rotated", chunk, 0, BANKS)
+        for b in range(BANKS):
+            add(nc.vector, 2 * HEADS - 1, slice(b * BANK, (b + 1) * BANK))
+            store(nc.sync, rotated_rows, "rotated", 2 * HEADS - 1, b, b + 1)

@@ -27,7 +27,9 @@ CHUNK = HALF_J * N
 BANKS = HALF_J // BANK_J
 WORDS = D // 2
 OCTAVES = 16
+WRAPPED = 72
 OCTAVE = 8
+AHEAD = 2
 ROUND_MAGIC = 1.5 * 2.0**23
 
 FLOPS = 2 * T * D * HEADS * N
@@ -53,7 +55,13 @@ def tile_bdhlayer_pa_e_kernel(tc, x, encoder_words, encoder_scales, out_0, out_1
         warm = keep.tile([P, 1], F32)
         nc.scalar.activation(out=warm[:], in_=one[:], func=ACT.Sin)
 
+        exponent = keep.tile([P, OCTAVES], I32)
+        nc.gpsimd.iota(exponent[:], pattern=[[-1, OCTAVES]], base=127, channel_multiplier=0)
+        token_int = keep.tile([P, J], I32)
+        nc.gpsimd.iota(token_int[:], pattern=[[1, J]], base=0, channel_multiplier=J)
         nc.gpsimd.memset(w_scales[:].rearrange("p h n -> p (h n)").bitcast(F32), 0.0)
+        identity = keep.tile([P, P], F32)
+        make_identity(nc, identity[:])
 
         def load_x(pair):
             pair_j = slice(pair * BANK_J, (pair + 1) * BANK_J)
@@ -67,22 +75,15 @@ def tile_bdhlayer_pa_e_kernel(tc, x, encoder_words, encoder_scales, out_0, out_1
 
         load_x(0)
         load_x(1)
+        load_words(0, 1)
         for quadrant in range(4):
             nc.sync.dma_start(
                 out=w_scales[32 * quadrant : 32 * quadrant + 4, :, :].bitcast(I32),
                 in_=encoder_scales[:, 4 * quadrant : 4 * quadrant + 4, :].rearrange("h r n -> r h n").bitcast(I32),
             )
-        load_words(0, 1)
         load_x(2)
         load_x(3)
         load_words(1, HEADS)
-
-        token_int = keep.tile([P, J], I32)
-        nc.gpsimd.iota(token_int[:], pattern=[[1, J]], base=0, channel_multiplier=J)
-        exponent = keep.tile([P, OCTAVES], I32)
-        nc.gpsimd.iota(exponent[:], pattern=[[-1, OCTAVES]], base=127, channel_multiplier=0)
-        identity = keep.tile([P, P], F32)
-        make_identity(nc, identity[:])
 
         octave = keep.tile([P, OCTAVE], F32)
         for r in range(OCTAVE):
@@ -102,9 +103,8 @@ def tile_bdhlayer_pa_e_kernel(tc, x, encoder_words, encoder_scales, out_0, out_1
         nc.vector.tensor_copy(out=token[:], in_=token_int[:])
 
         table_shape = [P, J, PAIRS]
-        phase = keep.tile(table_shape, F32)
-        whole = keep.tile(table_shape, F32)
         frac = keep.tile(table_shape, F32)
+        whole = keep.tile([P, J, WRAPPED], F32)
         half_sin = keep.tile(table_shape, F32)
         twice_square = keep.tile(table_shape, F32)
         cos = keep.tile(table_shape, F32)
@@ -113,10 +113,10 @@ def tile_bdhlayer_pa_e_kernel(tc, x, encoder_words, encoder_scales, out_0, out_1
         codes = keep.tile([P, J * P], U32, align_bytes=64)
         scales = keep.tile([P, J * P], U8, align_bytes=64)
 
-        def make_phase(engine, js):
+        def make_phase(js):
             shape = [P, js.stop - js.start, PAIRS]
-            engine.tensor_tensor(
-                out=phase[:, js, :],
+            nc.vector.tensor_tensor(
+                out=frac[:, js, :],
                 in0=token[:, js].unsqueeze(2).to_broadcast(shape),
                 in1=turns[:].rearrange("p o r -> p (o r)").unsqueeze(1).to_broadcast(shape),
                 op=ALU.mult,
@@ -124,11 +124,11 @@ def tile_bdhlayer_pa_e_kernel(tc, x, encoder_words, encoder_scales, out_0, out_1
 
         def make_whole(js):
             nc.vector.tensor_scalar(
-                out=whole[:, js, :], in0=phase[:, js, :], scalar1=ROUND_MAGIC, scalar2=ROUND_MAGIC, op0=ALU.add, op1=ALU.subtract
+                out=whole[:, js, :], in0=frac[:, js, 0:WRAPPED], scalar1=ROUND_MAGIC, scalar2=ROUND_MAGIC, op0=ALU.add, op1=ALU.subtract
             )
 
-        def make_frac(engine, js):
-            engine.tensor_tensor(out=frac[:, js, :], in0=phase[:, js, :], in1=whole[:, js, :], op=ALU.subtract)
+        def make_frac(js):
+            nc.vector.tensor_tensor(out=frac[:, js, 0:WRAPPED], in0=frac[:, js, 0:WRAPPED], in1=whole[:, js, :], op=ALU.subtract)
 
         def table_steps(js):
             return (
@@ -166,20 +166,20 @@ def tile_bdhlayer_pa_e_kernel(tc, x, encoder_words, encoder_scales, out_0, out_1
             )
 
         pair_0, pair_1, half_1 = slice(0, 2), slice(2, 4), slice(HALF_J, J)
-        make_phase(nc.vector, pair_0)
+        make_phase(pair_0)
+        make_phase(pair_1)
         make_whole(pair_0)
-        make_frac(nc.vector, pair_0)
+        make_whole(pair_1)
+        make_frac(pair_0)
+        make_frac(pair_1)
         for step in table_steps(pair_0):
             step()
-        make_phase(nc.vector, pair_1)
-        make_phase(nc.gpsimd, half_1)
+        make_phase(half_1)
         flip_x(0, nc.vector.tensor_copy)
-        make_whole(pair_1)
-        quantise_x(0, 1)
-        make_frac(nc.vector, pair_1)
-        flip_x(1, nc.scalar.copy)
         make_whole(half_1)
-        make_frac(nc.gpsimd, half_1)
+        quantise_x(0, 1)
+        make_frac(half_1)
+        flip_x(1, nc.scalar.copy)
         quantise_x(1, 2)
         for step in table_steps(pair_1):
             step()
@@ -206,24 +206,15 @@ def tile_bdhlayer_pa_e_kernel(tc, x, encoder_words, encoder_scales, out_0, out_1
                 in_=tiles[kind, chunk][:, first_bank * BANK : last_bank * BANK].rearrange("p (j n) -> p j n", n=N),
             )
 
-        for bank in range(all_banks):
+        def multiply(bank):
             chunk, b = divmod(bank, BANKS)
             half, head = divmod(chunk, HEADS)
-            by_bank = chunk == 0 or chunk >= 2 * HEADS - 2
-            if b == 0:
-                tiles["sparse", chunk] = results.tile([P, CHUNK], F32, name="sparse")
-                tiles["with_cos", chunk] = products.tile([P, CHUNK], F32, name="with_cos")
-                tiles["with_sin", chunk] = products.tile([P, CHUNK], F32, name="with_sin")
-                tiles["rotated", chunk] = results.tile([P, CHUNK], F32, name="rotated")
-            if bank == 6:
-                quantise_x(2, 4)
-
-            latent = psum_acc.tile([P, BANK], F32, name="latent")
+            tiles["latent", bank] = psum_acc.tile([P, BANK], F32, name="latent")
             for jj in range(BANK_J):
                 j = half * HALF_J + b * BANK_J + jj
                 tokens = slice(j * P, (j + 1) * P)
                 nc.tensor.matmul_mx(
-                    out=latent[:, jj * N : (jj + 1) * N],
+                    out=tiles["latent", bank][:, jj * N : (jj + 1) * N],
                     lhsT=codes[:, tokens].bitcast(FP8X4),
                     lhsT_scale=scales[:, tokens],
                     rhs=w_words[:, head, :].bitcast(FP8X4),
@@ -231,6 +222,25 @@ def tile_bdhlayer_pa_e_kernel(tc, x, encoder_words, encoder_scales, out_0, out_1
                     start=True,
                     stop=True,
                 )
+
+        for bank in range(AHEAD):
+            multiply(bank)
+
+        gpsimd_chunks = 2 * HEADS - 2
+        for bank in range(all_banks):
+            chunk, b = divmod(bank, BANKS)
+            half, head = divmod(chunk, HEADS)
+            if b == 0:
+                tiles["sparse", chunk] = results.tile([P, CHUNK], F32, name="sparse")
+                tiles["with_cos", chunk] = products.tile([P, CHUNK], F32, name="with_cos")
+                tiles["with_sin", chunk] = products.tile([P, CHUNK], F32, name="with_sin")
+                tiles["rotated", chunk] = results.tile([P, CHUNK], F32, name="rotated")
+            if bank == 2 * BANKS:
+                quantise_x(2, 4)
+            if bank + AHEAD < all_banks:
+                multiply(bank + AHEAD)
+
+            latent = tiles["latent", bank]
             columns = slice(b * BANK, (b + 1) * BANK)
             bank_j = slice(half * HALF_J + b * BANK_J, half * HALF_J + (b + 1) * BANK_J)
             latent_pairs = latent[:].rearrange("p (q c) -> p q c", c=2)
@@ -251,20 +261,20 @@ def tile_bdhlayer_pa_e_kernel(tc, x, encoder_words, encoder_scales, out_0, out_1
                 op1=ALU.mult,
             )
             nc.scalar.activation(out=tiles["sparse", chunk][:, columns], in_=latent[:], func=ACT.Relu)
-            if by_bank:
+            if chunk == 0 or chunk == 2 * HEADS - 1:
                 store(nc.scalar, sparse_rows, "sparse", chunk, b, b + 1)
             elif b == BANKS - 1:
                 store(nc.scalar, sparse_rows, "sparse", chunk, 0, BANKS)
-            if 1 <= bank <= len(scalar_extras):
-                scalar_extras[bank - 1]()
+            if bank < len(scalar_extras):
+                scalar_extras[bank]()
 
-            if chunk < 2 * HEADS - 1:
-                if by_bank:
-                    add(nc.gpsimd, chunk, columns)
-                    store(nc.sync, rotated_rows, "rotated", chunk, b, b + 1)
-                elif b == BANKS - 1:
-                    add(nc.gpsimd, chunk, slice(0, CHUNK))
-                    store(nc.sync, rotated_rows, "rotated", chunk, 0, BANKS)
-        for b in range(BANKS):
-            add(nc.vector, 2 * HEADS - 1, slice(b * BANK, (b + 1) * BANK))
-            store(nc.sync, rotated_rows, "rotated", 2 * HEADS - 1, b, b + 1)
+            if chunk == 0:
+                add(nc.gpsimd, chunk, columns)
+                store(nc.sync, rotated_rows, "rotated", chunk, b, b + 1)
+            elif chunk < gpsimd_chunks and b == BANKS - 1:
+                add(nc.gpsimd, chunk, slice(0, CHUNK))
+                store(nc.sync, rotated_rows, "rotated", chunk, 0, BANKS)
+        for chunk in range(gpsimd_chunks, 2 * HEADS):
+            for b in range(BANKS):
+                add(nc.vector, chunk, slice(b * BANK, (b + 1) * BANK))
+                store(nc.sync, rotated_rows, "rotated", chunk, b, b + 1)

import math
from contextlib import ExitStack

import concourse.mybir as mybir
from concourse.masks import make_identity

F32 = mybir.dt.float32
BF16 = mybir.dt.bfloat16
I32 = mybir.dt.int32
U32 = mybir.dt.uint32
U8 = mybir.dt.uint8
FP8X4 = mybir.dt.float8_e4m3fn_x4
ALU = mybir.AluOpType
ACT = mybir.ActivationFunctionType

P = 128
T = 1024
D = 512
HEADS = 6
N = 256
PAIRS = N // 2
J = T // P
HALF_J = J // 2
BANK_J = 2
BANK = BANK_J * N
CHUNK = HALF_J * N
BANKS = HALF_J // BANK_J
WORDS = D // 2
OCTAVES = 16
WRAPPED = 72
OCTAVE = 8
AHEAD = 2
ROUND_MAGIC = 1.5 * 2.0**23

FLOPS = 2 * T * D * HEADS * N


def tile_bdhlayer_pa_e_kernel(tc, x, encoder_words, encoder_scales, out_0, out_1):
    nc = tc.nc
    with ExitStack() as ctx:
        keep = ctx.enter_context(tc.tile_pool(name="keep", bufs=1))
        products = ctx.enter_context(tc.tile_pool(name="products", bufs=4))
        results = ctx.enter_context(tc.tile_pool(name="results", bufs=6))
        psum_t = ctx.enter_context(tc.psum_pool(name="psum_t", bufs=2))
        psum_acc = ctx.enter_context(tc.psum_pool(name="psum_acc", bufs=6))
        ctx.enter_context(tc.manual_schedule())

        x_rows = x[0, 0].rearrange("(p j) k -> p j k", j=J)
        x_sb = keep.tile([P, J, D], BF16)
        w_words = keep.tile([P, HEADS, N], U32, align_bytes=64)
        w_scales = keep.tile([P, HEADS, N], U8, align_bytes=64)

        one = keep.tile([P, 1], F32)
        nc.vector.memset(one[:], 1.0)
        warm = keep.tile([P, 1], F32)
        nc.scalar.activation(out=warm[:], in_=one[:], func=ACT.Sin)

        exponent = keep.tile([P, OCTAVES], I32)
        nc.gpsimd.iota(exponent[:], pattern=[[-1, OCTAVES]], base=127, channel_multiplier=0)
        token_int = keep.tile([P, J], I32)
        nc.gpsimd.iota(token_int[:], pattern=[[1, J]], base=0, channel_multiplier=J)
        nc.gpsimd.memset(w_scales[:].rearrange("p h n -> p (h n)").bitcast(F32), 0.0)
        identity = keep.tile([P, P], F32)
        make_identity(nc, identity[:])

        def load_x(pair):
            pair_j = slice(pair * BANK_J, (pair + 1) * BANK_J)
            nc.sync.dma_start(out=x_sb[:, pair_j, :], in_=x_rows[:, pair_j, :])

        def load_words(first, last):
            nc.sync.dma_start(
                out=w_words[:, first:last, :].bitcast(I32),
                in_=encoder_words[first:last].rearrange("h p n t -> p h (n t)").bitcast(I32),
            )

        load_x(0)
        load_x(1)
        load_words(0, 1)
        for quadrant in range(4):
            nc.sync.dma_start(
                out=w_scales[32 * quadrant : 32 * quadrant + 4, :, :].bitcast(I32),
                in_=encoder_scales[:, 4 * quadrant : 4 * quadrant + 4, :].rearrange("h r n -> r h n").bitcast(I32),
            )
        load_x(2)
        load_x(3)
        load_words(1, HEADS)

        octave = keep.tile([P, OCTAVE], F32)
        for r in range(OCTAVE):
            nc.vector.tensor_scalar_mul(
                out=octave[:, r : r + 1], in0=one[:], scalar1=2.0 ** (-r / OCTAVE) / (2.0 * math.pi)
            )
        halvings = keep.tile([P, OCTAVES], I32)
        nc.vector.tensor_single_scalar(out=halvings[:], in_=exponent[:], scalar=23, op=ALU.logical_shift_left)
        turns = keep.tile([P, OCTAVES, OCTAVE], F32)
        nc.vector.tensor_tensor(
            out=turns[:],
            in0=halvings[:].bitcast(F32).unsqueeze(2).to_broadcast([P, OCTAVES, OCTAVE]),
            in1=octave[:].unsqueeze(1).to_broadcast([P, OCTAVES, OCTAVE]),
            op=ALU.mult,
        )
        token = keep.tile([P, J], F32)
        nc.vector.tensor_copy(out=token[:], in_=token_int[:])

        table_shape = [P, J, PAIRS]
        frac = keep.tile(table_shape, F32)
        whole = keep.tile([P, J, WRAPPED], F32)
        half_sin = keep.tile(table_shape, F32)
        twice_square = keep.tile(table_shape, F32)
        cos = keep.tile(table_shape, F32)
        sines = keep.tile([P, 2, J, PAIRS], F32)
        grouped = keep.tile([P, J, P, 4], BF16, align_bytes=64)
        codes = keep.tile([P, J * P], U32, align_bytes=64)
        scales = keep.tile([P, J * P], U8, align_bytes=64)

        def make_phase(js):
            shape = [P, js.stop - js.start, PAIRS]
            nc.vector.tensor_tensor(
                out=frac[:, js, :],
                in0=token[:, js].unsqueeze(2).to_broadcast(shape),
                in1=turns[:].rearrange("p o r -> p (o r)").unsqueeze(1).to_broadcast(shape),
                op=ALU.mult,
            )

        def make_whole(js):
            nc.vector.tensor_scalar(
                out=whole[:, js, :], in0=frac[:, js, 0:WRAPPED], scalar1=ROUND_MAGIC, scalar2=ROUND_MAGIC, op0=ALU.add, op1=ALU.subtract
            )

        def make_frac(js):
            nc.vector.tensor_tensor(out=frac[:, js, 0:WRAPPED], in0=frac[:, js, 0:WRAPPED], in1=whole[:, js, :], op=ALU.subtract)

        def table_steps(js):
            return (
                lambda: nc.scalar.activation(out=half_sin[:, js, :], in_=frac[:, js, :], func=ACT.Sin, scale=math.pi),
                lambda: nc.scalar.activation(out=sines[:, 0, js, :], in_=frac[:, js, :], func=ACT.Sin, scale=-2.0 * math.pi),
                lambda: nc.scalar.activation(
                    out=twice_square[:, js, :], in_=half_sin[:, js, :], func=ACT.Square, scale=math.sqrt(2.0)
                ),
                lambda: nc.scalar.activation(out=sines[:, 1, js, :], in_=frac[:, js, :], func=ACT.Sin, scale=2.0 * math.pi),
                lambda: nc.scalar.activation(out=cos[:, js, :], in_=twice_square[:, js, :], func=ACT.Copy, scale=-1.0, bias=1.0),
            )

        x_words = x_sb[:].rearrange("p j k -> p (j k)").bitcast(F32)
        grouped_words = grouped[:].rearrange("q j t e -> q (j t e)").bitcast(F32).rearrange("q (j t u) -> q j t u", j=J, u=2)

        def flip_x(pair, copy):
            flipped = psum_t.tile([P, BANK_J, 2, P], F32, name="flipped")
            for jj in range(BANK_J):
                first = (pair * BANK_J + jj) * WORDS
                for u in range(2):
                    nc.tensor.transpose(
                        out=flipped[:, jj, u, :], in_=x_words[:, first + u : first + WORDS : 2], identity=identity[:]
                    )
            copy(
                out=grouped_words[:, pair * BANK_J : (pair + 1) * BANK_J, :, :],
                in_=flipped[:].rearrange("q j u t -> q j t u"),
            )

        def quantise_x(first_pair, last_pair):
            tokens = slice(first_pair * BANK_J * P, last_pair * BANK_J * P)
            nc.vector.quantize_mx(
                out=codes[:, tokens].bitcast(FP8X4),
                scales=scales[:, tokens],
                in_=grouped[:, first_pair * BANK_J : last_pair * BANK_J, :, :].rearrange("q j t e -> q (j t e)"),
            )

        pair_0, pair_1, half_1 = slice(0, 2), slice(2, 4), slice(HALF_J, J)
        make_phase(pair_0)
        make_phase(pair_1)
        make_whole(pair_0)
        make_whole(pair_1)
        make_frac(pair_0)
        make_frac(pair_1)
        for step in table_steps(pair_0):
            step()
        make_phase(half_1)
        flip_x(0, nc.vector.tensor_copy)
        make_whole(half_1)
        quantise_x(0, 1)
        make_frac(half_1)
        flip_x(1, nc.scalar.copy)
        quantise_x(1, 2)
        for step in table_steps(pair_1):
            step()

        sparse_rows = out_0[0].rearrange("h (p j) n -> h p j n", j=J)
        rotated_rows = out_1[0].rearrange("h (p j) n -> h p j n", j=J)
        all_banks = 2 * HEADS * BANKS
        scalar_extras = (lambda: flip_x(2, nc.scalar.copy), lambda: flip_x(3, nc.scalar.copy)) + table_steps(half_1)
        tiles = {}

        def add(engine, chunk, columns):
            engine.tensor_tensor(
                out=tiles["rotated", chunk][:, columns],
                in0=tiles["with_cos", chunk][:, columns],
                in1=tiles["with_sin", chunk][:, columns],
                op=ALU.add,
            )

        def store(queue, rows, kind, chunk, first_bank, last_bank):
            half, head = divmod(chunk, HEADS)
            nc_j = slice(half * HALF_J + first_bank * BANK_J, half * HALF_J + last_bank * BANK_J)
            queue.dma_start(
                out=rows[head][:, nc_j, :],
                in_=tiles[kind, chunk][:, first_bank * BANK : last_bank * BANK].rearrange("p (j n) -> p j n", n=N),
            )

        def multiply(bank):
            chunk, b = divmod(bank, BANKS)
            half, head = divmod(chunk, HEADS)
            tiles["latent", bank] = psum_acc.tile([P, BANK], F32, name="latent")
            for jj in range(BANK_J):
                j = half * HALF_J + b * BANK_J + jj
                tokens = slice(j * P, (j + 1) * P)
                nc.tensor.matmul_mx(
                    out=tiles["latent", bank][:, jj * N : (jj + 1) * N],
                    lhsT=codes[:, tokens].bitcast(FP8X4),
                    lhsT_scale=scales[:, tokens],
                    rhs=w_words[:, head, :].bitcast(FP8X4),
                    rhs_scale=w_scales[:, head, :],
                    start=True,
                    stop=True,
                )

        for bank in range(AHEAD):
            multiply(bank)

        gpsimd_chunks = 2 * HEADS - 2
        for bank in range(all_banks):
            chunk, b = divmod(bank, BANKS)
            half, head = divmod(chunk, HEADS)
            if b == 0:
                tiles["sparse", chunk] = results.tile([P, CHUNK], F32, name="sparse")
                tiles["with_cos", chunk] = products.tile([P, CHUNK], F32, name="with_cos")
                tiles["with_sin", chunk] = products.tile([P, CHUNK], F32, name="with_sin")
                tiles["rotated", chunk] = results.tile([P, CHUNK], F32, name="rotated")
            if bank == 2 * BANKS:
                quantise_x(2, 4)
            if bank + AHEAD < all_banks:
                multiply(bank + AHEAD)

            latent = tiles["latent", bank]
            columns = slice(b * BANK, (b + 1) * BANK)
            bank_j = slice(half * HALF_J + b * BANK_J, half * HALF_J + (b + 1) * BANK_J)
            latent_pairs = latent[:].rearrange("p (q c) -> p q c", c=2)
            nc.vector.scalar_tensor_tensor(
                out=tiles["with_cos", chunk][:, columns].rearrange("p (q c) -> p q c", c=2),
                in0=latent_pairs,
                scalar=0.0,
                in1=cos[:, bank_j, :].rearrange("p j i -> p (j i)").unsqueeze(2).to_broadcast([P, BANK // 2, 2]),
                op0=ALU.max,
                op1=ALU.mult,
            )
            nc.vector.scalar_tensor_tensor(
                out=tiles["with_sin", chunk][:, columns].rearrange("p (q c) -> p q c", c=2),
                in0=latent_pairs[:, :, ::-1],
                scalar=0.0,
                in1=sines[:, :, bank_j, :].rearrange("p c j i -> p (j i) c"),
                op0=ALU.max,
                op1=ALU.mult,
            )
            nc.scalar.activation(out=tiles["sparse", chunk][:, columns], in_=latent[:], func=ACT.Relu)
            if chunk == 0 or chunk == 2 * HEADS - 1:
                store(nc.scalar, sparse_rows, "sparse", chunk, b, b + 1)
            elif b == BANKS - 1:
                store(nc.scalar, sparse_rows, "sparse", chunk, 0, BANKS)
            if bank < len(scalar_extras):
                scalar_extras[bank]()

            if chunk == 0:
                add(nc.gpsimd, chunk, columns)
                store(nc.sync, rotated_rows, "rotated", chunk, b, b + 1)
            elif chunk < gpsimd_chunks and b == BANKS - 1:
                add(nc.gpsimd, chunk, slice(0, CHUNK))
                store(nc.sync, rotated_rows, "rotated", chunk, 0, BANKS)
        for chunk in range(gpsimd_chunks, 2 * HEADS):
            for b in range(BANKS):
                add(nc.vector, chunk, slice(b * BANK, (b + 1) * BANK))
                store(nc.sync, rotated_rows, "rotated", chunk, b, b + 1)
